import numpy as np
import ml_dtypes


def mxq(x, axis, fmt="e4m3"):
    dtype, down = {"e4m3": (ml_dtypes.float8_e4m3fn, 7), "e5m2": (ml_dtypes.float8_e5m2, 14)}[fmt]
    v = np.moveaxis(np.asarray(x, np.float32).astype(ml_dtypes.bfloat16).astype(np.float64), axis, -1)
    blocks = v.reshape(v.shape[:-1] + (-1, 32))
    amax = np.abs(blocks).max(-1, keepdims=True)
    byte = np.maximum(np.where(amax > 0, np.frexp(amax)[1] - 1 + 127, 0) - down, 1)
    scale = np.exp2(byte - 127.0)
    codes = (blocks / scale).astype(np.float32).astype(dtype).astype(np.float64)
    return np.moveaxis((codes * scale).reshape(v.shape), -1, axis)


WIDE = False


def mx_kscale(k):
    if not WIDE:
        return np.ones(k)
    levels = np.array([20, -20, 10, -10, 0])
    a = np.random.permutation(np.resize(levels, k // 512 * 4)).reshape(k // 512, 4)
    idx = np.arange(k)
    return np.exp2(a[idx // 512, idx % 128 // 32])


BF16 = ml_dtypes.bfloat16


def bf(x):
    return np.asarray(x, np.float32).astype(BF16)


def f64(x):
    return np.asarray(x).astype(np.float64)


B, F, G, N, L = 512, 512, 512, 100, 2
S2 = (L + 1) ** 2
C2 = sum((2 * k + 1) ** 2 for k in range(L + 1))


def setup_inputs():
    u = mx_kscale(G)[:, None, None]
    x = np.random.standard_normal((B, F, S2))
    psi = np.random.standard_normal((G, F, S2)) / u
    g = np.random.standard_normal((G, B, C2)) * np.exp2(np.random.randint(-12, 1, (1, B, 1))) * 8.0 * u
    return {"x": bf(x), "psi": bf(psi), "grad_out": bf(g)}


def reference(x, psi, grad_out):
    gq = mxq(f64(grad_out), 0, "e5m2")
    pq = mxq(f64(psi), 0, "e4m3")
    scale = 1.0 / np.sqrt(F)
    gx = np.zeros((B, F, S2))
    c = 0
    for l in range(L + 1):
        s, d = l * l, 2 * l + 1
        a = gq[:, :, c:c + d * d].reshape(G, B, d, d).transpose(1, 2, 3, 0).reshape(B * d, d * G)
        p = pq[:, :, s:s + d].transpose(2, 0, 1).reshape(d * G, F)
        o = scale * (a @ p)
        gx[:, :, s:s + d] = o.reshape(B, d, F).transpose(0, 2, 1)
        c += d * d
    return gx

@@ -1,0 +1,133 @@
+import math
+from contextlib import ExitStack
+
+import concourse.mybir as mybir
+
+BF16 = mybir.dt.bfloat16
+F32 = mybir.dt.float32
+U32 = mybir.dt.uint32
+U8 = mybir.dt.uint8
+E4M3_X4 = mybir.dt.float8_e4m3fn_x4
+E5M2_X4 = mybir.dt.float8_e5m2_x4
+
+P = 128
+PACK = 4
+OUT_FEATURES = 512
+BATCH = 512
+IN_FEATURES = 512
+DEGREES = 3
+COEFFS = 9
+BLOCKS = 35
+COLS = 128
+RUN = 4
+
+SCALE = 1.0 / math.sqrt(IN_FEATURES)
+FLOPS = 2 * OUT_FEATURES * BATCH * IN_FEATURES * BLOCKS
+BYTES = 2 * OUT_FEATURES * (IN_FEATURES * COEFFS + BATCH * BLOCKS) + 4 * BATCH * IN_FEATURES * COEFFS
+
+
+def products():
+    rows = []
+    for degree in range(DEGREES):
+        d = 2 * degree + 1
+        s = degree * degree
+        for u in range(d):
+            for m in range(d):
+                rows.append((s + u, s + m, m == 0, m == d - 1))
+    return rows
+
+
+def plane_groups(planes):
+    return [(first, min(RUN, planes - first)) for first in range(0, planes, RUN)]
+
+
+def regroup(engine_copy, pool, raw, first, count):
+    grouped = pool.tile([P, RUN, COLS, PACK], BF16, align_bytes=64, name="grouped")
+    engine_copy(
+        out=grouped[:, 0:count].rearrange("p j c t -> p c t j"),
+        in_=raw[:, :, :, first : first + count].rearrange("p t c j -> p c t j"),
+    )
+    return grouped
+
+
+def tile_s2conv_pa_kernel(tc, x, psi, grad_out, out):
+    nc = tc.nc
+    psi_rows = psi.rearrange("(p t) f c -> p t f c", t=PACK)
+    grad_rows = grad_out.rearrange("(p t) b j -> p t b j", t=PACK)
+    copiers = [nc.vector.tensor_copy, nc.scalar.copy]
+
+    with ExitStack() as ctx:
+        keep = ctx.enter_context(tc.tile_pool(name="keep", bufs=1))
+        grad_in = ctx.enter_context(tc.tile_pool(name="grad_in", bufs=3))
+        group_pool = ctx.enter_context(tc.tile_pool(name="group_pool", bufs=6))
+        code_pool = ctx.enter_context(tc.tile_pool(name="code_pool", bufs=6))
+        psum = ctx.enter_context(tc.psum_pool(name="psum", bufs=6))
+
+        psi_codes = keep.tile([P, COEFFS, IN_FEATURES], U32, align_bytes=64)
+        psi_scales = keep.tile([P, COEFFS, IN_FEATURES], U8, align_bytes=64)
+        copies = 0
+        with tc.tile_pool(name="psi_in", bufs=IN_FEATURES // COLS) as psi_in:
+            for chunk in range(IN_FEATURES // COLS):
+                cols = slice(chunk * COLS, (chunk + 1) * COLS)
+                psi_raw = psi_in.tile([P, PACK, COLS, COEFFS], BF16)
+                nc.sync.dma_start(out=psi_raw[:], in_=psi_rows[:, :, cols, :])
+                for first, count in plane_groups(COEFFS):
+                    grouped = regroup(copiers[copies % 2], group_pool, psi_raw, first, count)
+                    copies += 1
+                    for i in range(count):
+                        nc.vector.quantize_mx(
+                            out=psi_codes[:, first + i, cols].bitcast(E4M3_X4),
+                            scales=psi_scales[:, first + i, cols],
+                            in_=grouped[:, i].rearrange("p c t -> p (c t)"),
+                        )
+
+        plane_pool = ctx.enter_context(tc.tile_pool(name="plane_pool", bufs=2))
+        out_pool = ctx.enter_context(tc.tile_pool(name="out_pool", bufs=4))
+        table = products()
+        for batch_tile in range(BATCH // COLS):
+            rows = slice(batch_tile * COLS, (batch_tile + 1) * COLS)
+            grad_raw = grad_in.tile([P, PACK, COLS, BLOCKS], BF16)
+            nc.sync.dma_start(out=grad_raw[:], in_=grad_rows[:, :, rows, :])
+            planes = plane_pool.tile([P, COEFFS, IN_FEATURES], F32)
+            for first, count in plane_groups(BLOCKS):
+                grouped = regroup(copiers[copies % 2], group_pool, grad_raw, first, count)
+                copies += 1
+                codes = code_pool.tile([P, RUN, COLS], U32, align_bytes=64)
+                scales = code_pool.tile([P, RUN, COLS], U8, align_bytes=64)
+                done = 0
+                for width in (4, 2, 1):
+                    if count - done >= width:
+                        part = slice(done, done + width)
+                        nc.vector.quantize_mx(
+                            out=codes[:, part].rearrange("p j c -> p (j c)").bitcast(E5M2_X4),
+                            scales=scales[:, part].rearrange("p j c -> p (j c)"),
+                            in_=grouped[:, part].rearrange("p j c t -> p (j c t)"),
+                        )
+                        done += width
+                for i in range(count):
+                    coefficient, psi_plane, opens, closes = table[first + i]
+                    if opens:
+                        acc = psum.tile([P, IN_FEATURES], F32)
+                    nc.tensor.matmul_mx(
+                        out=acc[:],
+                        lhsT=codes[:, i].bitcast(E5M2_X4),
+                        lhsT_scale=scales[:, i],
+                        rhs=psi_codes[:, psi_plane].bitcast(E4M3_X4),
+                        rhs_scale=psi_scales[:, psi_plane],
+                        start=opens,
+                        stop=closes,
+                    )
+                    if closes:
+                        nc.scalar.activation(
+                            out=planes[:, coefficient],
+                            in_=acc[:],
+                            func=mybir.ActivationFunctionType.Copy,
+                            scale=SCALE,
+                        )
+            for chunk in range(IN_FEATURES // COLS):
+                cols = slice(chunk * COLS, (chunk + 1) * COLS)
+                woven = out_pool.tile([P, COLS, COEFFS], F32)
+                nc.vector.tensor_copy(
+                    out=woven[:], in_=planes[:, :, cols].rearrange("p c f -> p f c")
+                )
+                nc.sync.dma_start(out=out[rows, cols, :], in_=woven[:])

@@ -128,6 +128,7 @@ def tile_s2conv_pa_kernel(tc, x, psi, grad_out, out):
                 cols = slice(chunk * COLS, (chunk + 1) * COLS)
                 woven = out_pool.tile([P, COLS, COEFFS], F32)
                 nc.vector.tensor_copy(
-                    out=woven[:], in_=planes[:, :, cols].rearrange("p c f -> p f c")
+                    out=woven[:].rearrange("p (n i) c -> p n c i", i=RUN),
+                    in_=planes[:, :, cols].rearrange("p c (n i) -> p n c i", i=RUN),
                 )
                 nc.sync.dma_start(out=out[rows, cols, :], in_=woven[:])

@@ -20,6 +20,9 @@ COEFFS = 9
 BLOCKS = 35
 COLS = 128
 RUN = 4
+QUANTISE_LAG = 2
+EMPTY_LAG = 4
+AHEAD = 2
 
 SCALE = 1.0 / math.sqrt(IN_FEATURES)
 FLOPS = 2 * OUT_FEATURES * BATCH * IN_FEATURES * BLOCKS
@@ -41,94 +44,149 @@ def plane_groups(planes):
     return [(first, min(RUN, planes - first)) for first in range(0, planes, RUN)]
 
 
-def regroup(engine_copy, pool, raw, first, count):
-    grouped = pool.tile([P, RUN, COLS, PACK], BF16, align_bytes=64, name="grouped")
-    engine_copy(
-        out=grouped[:, 0:count].rearrange("p j c t -> p c t j"),
-        in_=raw[:, :, :, first : first + count].rearrange("p t c j -> p c t j"),
-    )
-    return grouped
-
-
 def tile_s2conv_pa_kernel(tc, x, psi, grad_out, out):
     nc = tc.nc
     psi_rows = psi.rearrange("(p t) f c -> p t f c", t=PACK)
     grad_rows = grad_out.rearrange("(p t) b j -> p t b j", t=PACK)
-    copiers = [nc.vector.tensor_copy, nc.scalar.copy]
+    chunks = IN_FEATURES // COLS
+    batch_tiles = BATCH // COLS
 
     with ExitStack() as ctx:
+        ctx.enter_context(tc.manual_schedule())
         keep = ctx.enter_context(tc.tile_pool(name="keep", bufs=1))
-        grad_in = ctx.enter_context(tc.tile_pool(name="grad_in", bufs=3))
+        grad_in = ctx.enter_context(tc.tile_pool(name="grad_in", bufs=AHEAD + 1))
         group_pool = ctx.enter_context(tc.tile_pool(name="group_pool", bufs=6))
-        code_pool = ctx.enter_context(tc.tile_pool(name="code_pool", bufs=6))
-        psum = ctx.enter_context(tc.psum_pool(name="psum", bufs=6))
+        code_pool = ctx.enter_context(tc.tile_pool(name="code_pool", bufs=4))
+        psum = ctx.enter_context(tc.psum_pool(name="psum", bufs=8))
+
+        def regroup(step, raw, first, count):
+            grouped = group_pool.tile([P, RUN, COLS, PACK], BF16, align_bytes=64)
+            copy = nc.vector.tensor_copy if step % 2 == 0 else nc.scalar.copy
+            copy(
+                out=grouped[:, 0:count].rearrange("p j c t -> p c t j"),
+                in_=raw[:, :, :, first : first + count].rearrange("p t c j -> p c t j"),
+            )
+            return grouped
+
+        def load_grad(batch_tile):
+            grad_raw = grad_in.tile([P, PACK, COLS, BLOCKS], BF16)
+            rows = slice(batch_tile * COLS, (batch_tile + 1) * COLS)
+            nc.sync.dma_start(out=grad_raw[:], in_=grad_rows[:, :, rows, :])
+            return grad_raw
 
         psi_codes = keep.tile([P, COEFFS, IN_FEATURES], U32, align_bytes=64)
         psi_scales = keep.tile([P, COEFFS, IN_FEATURES], U8, align_bytes=64)
-        copies = 0
-        with tc.tile_pool(name="psi_in", bufs=IN_FEATURES // COLS) as psi_in:
-            for chunk in range(IN_FEATURES // COLS):
-                cols = slice(chunk * COLS, (chunk + 1) * COLS)
+        grad_raws = {}
+        grouped_of = {}
+        with tc.tile_pool(name="psi_in", bufs=chunks) as psi_in:
+            psi_raws = []
+            for chunk in range(chunks):
                 psi_raw = psi_in.tile([P, PACK, COLS, COEFFS], BF16)
+                cols = slice(chunk * COLS, (chunk + 1) * COLS)
                 nc.sync.dma_start(out=psi_raw[:], in_=psi_rows[:, :, cols, :])
-                for first, count in plane_groups(COEFFS):
-                    grouped = regroup(copiers[copies % 2], group_pool, psi_raw, first, count)
-                    copies += 1
-                    for i in range(count):
+                psi_raws.append(psi_raw)
+            for batch_tile in range(AHEAD):
+                grad_raws[batch_tile] = load_grad(batch_tile)
+
+            psi_steps = [
+                (chunk, first, count)
+                for chunk in range(chunks)
+                for first, count in plane_groups(COEFFS)
+            ]
+            for i in range(len(psi_steps) + QUANTISE_LAG):
+                if i < len(psi_steps):
+                    chunk, first, count = psi_steps[i]
+                    grouped_of[i] = regroup(i, psi_raws[chunk], first, count)
+                q = i - QUANTISE_LAG
+                if q >= 0:
+                    chunk, first, count = psi_steps[q]
+                    cols = slice(chunk * COLS, (chunk + 1) * COLS)
+                    for n in range(count):
                         nc.vector.quantize_mx(
-                            out=psi_codes[:, first + i, cols].bitcast(E4M3_X4),
-                            scales=psi_scales[:, first + i, cols],
-                            in_=grouped[:, i].rearrange("p c t -> p (c t)"),
+                            out=psi_codes[:, first + n, cols].bitcast(E4M3_X4),
+                            scales=psi_scales[:, first + n, cols],
+                            in_=grouped_of[q][:, n].rearrange("p c t -> p (c t)"),
                         )
 
         plane_pool = ctx.enter_context(tc.tile_pool(name="plane_pool", bufs=2))
         out_pool = ctx.enter_context(tc.tile_pool(name="out_pool", bufs=4))
         table = products()
-        for batch_tile in range(BATCH // COLS):
-            rows = slice(batch_tile * COLS, (batch_tile + 1) * COLS)
-            grad_raw = grad_in.tile([P, PACK, COLS, BLOCKS], BF16)
-            nc.sync.dma_start(out=grad_raw[:], in_=grad_rows[:, :, rows, :])
-            planes = plane_pool.tile([P, COEFFS, IN_FEATURES], F32)
-            for first, count in plane_groups(BLOCKS):
-                grouped = regroup(copiers[copies % 2], group_pool, grad_raw, first, count)
-                copies += 1
-                codes = code_pool.tile([P, RUN, COLS], U32, align_bytes=64)
-                scales = code_pool.tile([P, RUN, COLS], U8, align_bytes=64)
-                done = 0
-                for width in (4, 2, 1):
-                    if count - done >= width:
-                        part = slice(done, done + width)
-                        nc.vector.quantize_mx(
-                            out=codes[:, part].rearrange("p j c -> p (j c)").bitcast(E5M2_X4),
-                            scales=scales[:, part].rearrange("p j c -> p (j c)"),
-                            in_=grouped[:, part].rearrange("p j c t -> p (j c t)"),
-                        )
-                        done += width
-                for i in range(count):
-                    coefficient, psi_plane, opens, closes = table[first + i]
-                    if opens:
-                        acc = psum.tile([P, IN_FEATURES], F32)
-                    nc.tensor.matmul_mx(
-                        out=acc[:],
-                        lhsT=codes[:, i].bitcast(E5M2_X4),
-                        lhsT_scale=scales[:, i],
-                        rhs=psi_codes[:, psi_plane].bitcast(E4M3_X4),
-                        rhs_scale=psi_scales[:, psi_plane],
-                        start=opens,
-                        stop=closes,
+        groups = plane_groups(BLOCKS)
+        grad_steps = [
+            (batch_tile, first, count)
+            for batch_tile in range(batch_tiles)
+            for first, count in groups
+        ]
+        grouped_of = {}
+        bank_of = {}
+        planes_of = {}
+
+        def quantise_and_multiply(step):
+            batch_tile, first, count = grad_steps[step]
+            grouped = grouped_of[step]
+            codes = code_pool.tile([P, RUN, COLS], U32, align_bytes=64)
+            scales = code_pool.tile([P, RUN, COLS], U8, align_bytes=64)
+            done = 0
+            for width in (4, 2, 1):
+                if count - done >= width:
+                    part = slice(done, done + width)
+                    nc.vector.quantize_mx(
+                        out=codes[:, part].rearrange("p j c -> p (j c)").bitcast(E5M2_X4),
+                        scales=scales[:, part].rearrange("p j c -> p (j c)"),
+                        in_=grouped[:, part].rearrange("p j c t -> p (j c t)"),
                     )
-                    if closes:
-                        nc.scalar.activation(
-                            out=planes[:, coefficient],
-                            in_=acc[:],
-                            func=mybir.ActivationFunctionType.Copy,
-                            scale=SCALE,
-                        )
-            for chunk in range(IN_FEATURES // COLS):
-                cols = slice(chunk * COLS, (chunk + 1) * COLS)
-                woven = out_pool.tile([P, COLS, COEFFS], F32)
-                nc.vector.tensor_copy(
-                    out=woven[:].rearrange("p (n i) c -> p n c i", i=RUN),
-                    in_=planes[:, :, cols].rearrange("p c (n i) -> p n c i", i=RUN),
+                    done += width
+            for n in range(count):
+                coefficient, psi_plane, opens, closes = table[first + n]
+                if opens:
+                    bank = psum.tile([P, IN_FEATURES], F32)
+                    bank_of[(batch_tile, coefficient)] = bank
+                nc.tensor.matmul_mx(
+                    out=bank_of[(batch_tile, coefficient)][:],
+                    lhsT=codes[:, n].bitcast(E5M2_X4),
+                    lhsT_scale=scales[:, n],
+                    rhs=psi_codes[:, psi_plane].bitcast(E4M3_X4),
+                    rhs_scale=psi_scales[:, psi_plane],
+                    start=opens,
+                    stop=closes,
                 )
-                nc.sync.dma_start(out=out[rows, cols, :], in_=woven[:])
+
+        def empty_banks(step):
+            batch_tile, first, count = grad_steps[step]
+            if first == 0:
+                planes = plane_pool.tile([P, COEFFS, IN_FEATURES], F32)
+                planes_of[batch_tile] = planes
+            for n in range(count):
+                coefficient, psi_plane, opens, closes = table[first + n]
+                if closes:
+                    nc.scalar.activation(
+                        out=planes_of[batch_tile][:, coefficient],
+                        in_=bank_of[(batch_tile, coefficient)][:],
+                        func=mybir.ActivationFunctionType.Copy,
+                        scale=SCALE,
+                    )
+
+        def weave_and_store(batch_tile, chunk):
+            rows = slice(batch_tile * COLS, (batch_tile + 1) * COLS)
+            cols = slice(chunk * COLS, (chunk + 1) * COLS)
+            woven = out_pool.tile([P, COLS, COEFFS], F32)
+            nc.vector.tensor_copy(
+                out=woven[:].rearrange("p (n i) c -> p n c i", i=RUN),
+                in_=planes_of[batch_tile][:, :, cols].rearrange("p c (n i) -> p n c i", i=RUN),
+            )
+            nc.sync.dma_start(out=out[rows, cols, :], in_=woven[:])
+
+        for i in range(len(grad_steps) + EMPTY_LAG + chunks):
+            if i < len(grad_steps):
+                batch_tile, first, count = grad_steps[i]
+                if first == 0 and batch_tile + AHEAD < batch_tiles:
+                    grad_raws[batch_tile + AHEAD] = load_grad(batch_tile + AHEAD)
+                grouped_of[i] = regroup(i, grad_raws[batch_tile], first, count)
+            q = i - QUANTISE_LAG
+            if 0 <= q < len(grad_steps):
+                quantise_and_multiply(q)
+            e = i - EMPTY_LAG
+            if 0 <= e < len(grad_steps):
+                empty_banks(e)
+            if e >= len(groups) and e % len(groups) < chunks:
+                weave_and_store(e // len(groups) - 1, e % len(groups))

@@ -59,9 +59,9 @@ def tile_s2conv_pa_kernel(tc, x, psi, grad_out, out):
         code_pool = ctx.enter_context(tc.tile_pool(name="code_pool", bufs=4))
         psum = ctx.enter_context(tc.psum_pool(name="psum", bufs=8))
 
-        def regroup(step, raw, first, count):
+        def regroup(raw, first, count):
             grouped = group_pool.tile([P, RUN, COLS, PACK], BF16, align_bytes=64)
-            copy = nc.vector.tensor_copy if step % 2 == 0 else nc.scalar.copy
+            copy = nc.vector.tensor_copy if (first // RUN) % 2 == 0 else nc.scalar.copy
             copy(
                 out=grouped[:, 0:count].rearrange("p j c t -> p c t j"),
                 in_=raw[:, :, :, first : first + count].rearrange("p t c j -> p c t j"),
@@ -96,7 +96,7 @@ def tile_s2conv_pa_kernel(tc, x, psi, grad_out, out):
             for i in range(len(psi_steps) + QUANTISE_LAG):
                 if i < len(psi_steps):
                     chunk, first, count = psi_steps[i]
-                    grouped_of[i] = regroup(i, psi_raws[chunk], first, count)
+                    grouped_of[i] = regroup(psi_raws[chunk], first, count)
                 q = i - QUANTISE_LAG
                 if q >= 0:
                     chunk, first, count = psi_steps[q]
@@ -181,7 +181,7 @@ def tile_s2conv_pa_kernel(tc, x, psi, grad_out, out):
                 batch_tile, first, count = grad_steps[i]
                 if first == 0 and batch_tile + AHEAD < batch_tiles:
                     grad_raws[batch_tile + AHEAD] = load_grad(batch_tile + AHEAD)
-                grouped_of[i] = regroup(i, grad_raws[batch_tile], first, count)
+                grouped_of[i] = regroup(grad_raws[batch_tile], first, count)
             q = i - QUANTISE_LAG
             if 0 <= q < len(grad_steps):
                 quantise_and_multiply(q)

@@ -21,7 +21,7 @@ BLOCKS = 35
 COLS = 128
 RUN = 4
 QUANTISE_LAG = 2
-EMPTY_LAG = 4
+EMPTY_LAG = 2
 AHEAD = 2
 
 SCALE = 1.0 / math.sqrt(IN_FEATURES)
@@ -50,82 +50,85 @@ def tile_s2conv_pa_kernel(tc, x, psi, grad_out, out):
     grad_rows = grad_out.rearrange("(p t) b j -> p t b j", t=PACK)
     chunks = IN_FEATURES // COLS
     batch_tiles = BATCH // COLS
+    table = products()
+    halves = [slice(0, COLS // 2), slice(COLS // 2, COLS)]
+    whole = [slice(0, COLS)]
+
+    steps = []
+    copies = []
+    for is_grad, tiles, planes in ((False, chunks, COEFFS), (True, batch_tiles, BLOCKS)):
+        groups = plane_groups(planes)
+        for tile in range(tiles):
+            base = len(steps)
+            for first, count in groups:
+                steps.append((is_grad, tile, first, count))
+            for part in halves if tile == 0 else whole:
+                for n in range(len(groups)):
+                    if is_grad:
+                        on_vector = n % 2 == 0
+                    else:
+                        on_vector = n == 0
+                    copies.append((base + n, part, on_vector))
+    last_copy = {}
+    for n, (step, part, on_vector) in enumerate(copies):
+        last_copy[step] = n
+    psi_copies = sum(1 for step, part, on_vector in copies if not steps[step][0])
 
     with ExitStack() as ctx:
         ctx.enter_context(tc.manual_schedule())
         keep = ctx.enter_context(tc.tile_pool(name="keep", bufs=1))
         grad_in = ctx.enter_context(tc.tile_pool(name="grad_in", bufs=AHEAD + 1))
-        group_pool = ctx.enter_context(tc.tile_pool(name="group_pool", bufs=6))
+        group_pool = ctx.enter_context(tc.tile_pool(name="group_pool", bufs=10))
         code_pool = ctx.enter_context(tc.tile_pool(name="code_pool", bufs=4))
         psum = ctx.enter_context(tc.psum_pool(name="psum", bufs=8))
 
-        def regroup(raw, first, count):
-            grouped = group_pool.tile([P, RUN, COLS, PACK], BF16, align_bytes=64)
-            copy = nc.vector.tensor_copy if (first // RUN) % 2 == 0 else nc.scalar.copy
-            copy(
-                out=grouped[:, 0:count].rearrange("p j c t -> p c t j"),
-                in_=raw[:, :, :, first : first + count].rearrange("p t c j -> p c t j"),
-            )
-            return grouped
-
-        def load_grad(batch_tile):
-            grad_raw = grad_in.tile([P, PACK, COLS, BLOCKS], BF16)
-            rows = slice(batch_tile * COLS, (batch_tile + 1) * COLS)
-            nc.sync.dma_start(out=grad_raw[:], in_=grad_rows[:, :, rows, :])
-            return grad_raw
-
         psi_codes = keep.tile([P, COEFFS, IN_FEATURES], U32, align_bytes=64)
         psi_scales = keep.tile([P, COEFFS, IN_FEATURES], U8, align_bytes=64)
-        grad_raws = {}
-        grouped_of = {}
-        with tc.tile_pool(name="psi_in", bufs=chunks) as psi_in:
-            psi_raws = []
-            for chunk in range(chunks):
-                psi_raw = psi_in.tile([P, PACK, COLS, COEFFS], BF16)
-                cols = slice(chunk * COLS, (chunk + 1) * COLS)
-                nc.sync.dma_start(out=psi_raw[:], in_=psi_rows[:, :, cols, :])
-                psi_raws.append(psi_raw)
-            for batch_tile in range(AHEAD):
-                grad_raws[batch_tile] = load_grad(batch_tile)
 
-            psi_steps = [
-                (chunk, first, count)
-                for chunk in range(chunks)
-                for first, count in plane_groups(COEFFS)
-            ]
-            for i in range(len(psi_steps) + QUANTISE_LAG):
-                if i < len(psi_steps):
-                    chunk, first, count = psi_steps[i]
-                    grouped_of[i] = regroup(psi_raws[chunk], first, count)
-                q = i - QUANTISE_LAG
-                if q >= 0:
-                    chunk, first, count = psi_steps[q]
-                    cols = slice(chunk * COLS, (chunk + 1) * COLS)
-                    for n in range(count):
-                        nc.vector.quantize_mx(
-                            out=psi_codes[:, first + n, cols].bitcast(E4M3_X4),
-                            scales=psi_scales[:, first + n, cols],
-                            in_=grouped_of[q][:, n].rearrange("p c t -> p (c t)"),
-                        )
-
-        plane_pool = ctx.enter_context(tc.tile_pool(name="plane_pool", bufs=2))
-        out_pool = ctx.enter_context(tc.tile_pool(name="out_pool", bufs=4))
-        table = products()
-        groups = plane_groups(BLOCKS)
-        grad_steps = [
-            (batch_tile, first, count)
-            for batch_tile in range(batch_tiles)
-            for first, count in groups
-        ]
+        raw_of = {}
         grouped_of = {}
         bank_of = {}
         planes_of = {}
+        pools = {}
+
+        def load(is_grad, tile):
+            if is_grad:
+                raw = grad_in.tile([P, PACK, COLS, BLOCKS], BF16, name="grad_raw")
+                rows = grad_rows
+            else:
+                raw = pools["psi_in"].tile([P, PACK, COLS, COEFFS], BF16, name="psi_raw")
+                rows = psi_rows
+            raw_of[(is_grad, tile)] = raw
+            for part in halves if tile == 0 else whole:
+                cols = slice(tile * COLS + part.start, tile * COLS + part.stop)
+                nc.sync.dma_start(out=raw[:, :, part, :], in_=rows[:, :, cols, :])
+
+        def regroup(step, part, on_vector):
+            is_grad, tile, first, count = steps[step]
+            if step not in grouped_of:
+                grouped = group_pool.tile([P, RUN, COLS, PACK], BF16, align_bytes=64, name="grouped")
+                grouped_of[step] = grouped
+            copy = nc.vector.tensor_copy if on_vector else nc.scalar.copy
+            copy(
+                out=grouped_of[step][:, 0:count, part].rearrange("p j c t -> p c t j"),
+                in_=raw_of[(is_grad, tile)][:, :, part, first : first + count].rearrange("p t c j -> p c t j"),
+            )
+
+        def quantise_psi(step):
+            is_grad, chunk, first, count = steps[step]
+            cols = slice(chunk * COLS, (chunk + 1) * COLS)
+            for n in range(count):
+                nc.vector.quantize_mx(
+                    out=psi_codes[:, first + n, cols].bitcast(E4M3_X4),
+                    scales=psi_scales[:, first + n, cols],
+                    in_=grouped_of[step][:, n].rearrange("p c t -> p (c t)"),
+                )
 
         def quantise_and_multiply(step):
-            batch_tile, first, count = grad_steps[step]
+            is_grad, batch_tile, first, count = steps[step]
             grouped = grouped_of[step]
-            codes = code_pool.tile([P, RUN, COLS], U32, align_bytes=64)
-            scales = code_pool.tile([P, RUN, COLS], U8, align_bytes=64)
+            codes = code_pool.tile([P, RUN, COLS], U32, align_bytes=64, name="codes")
+            scales = code_pool.tile([P, RUN, COLS], U8, align_bytes=64, name="scales")
             done = 0
             for width in (4, 2, 1):
                 if count - done >= width:
@@ -139,7 +142,7 @@ def tile_s2conv_pa_kernel(tc, x, psi, grad_out, out):
             for n in range(count):
                 coefficient, psi_plane, opens, closes = table[first + n]
                 if opens:
-                    bank = psum.tile([P, IN_FEATURES], F32)
+                    bank = psum.tile([P, IN_FEATURES], F32, name="bank")
                     bank_of[(batch_tile, coefficient)] = bank
                 nc.tensor.matmul_mx(
                     out=bank_of[(batch_tile, coefficient)][:],
@@ -152,9 +155,9 @@ def tile_s2conv_pa_kernel(tc, x, psi, grad_out, out):
                 )
 
         def empty_banks(step):
-            batch_tile, first, count = grad_steps[step]
+            is_grad, batch_tile, first, count = steps[step]
             if first == 0:
-                planes = plane_pool.tile([P, COEFFS, IN_FEATURES], F32)
+                planes = pools["plane"].tile([P, COEFFS, IN_FEATURES], F32, name="planes")
                 planes_of[batch_tile] = planes
             for n in range(count):
                 coefficient, psi_plane, opens, closes = table[first + n]
@@ -169,24 +172,53 @@ def tile_s2conv_pa_kernel(tc, x, psi, grad_out, out):
         def weave_and_store(batch_tile, chunk):
             rows = slice(batch_tile * COLS, (batch_tile + 1) * COLS)
             cols = slice(chunk * COLS, (chunk + 1) * COLS)
-            woven = out_pool.tile([P, COLS, COEFFS], F32)
+            woven = pools["out"].tile([P, COLS, COEFFS], F32, name="woven")
             nc.vector.tensor_copy(
                 out=woven[:].rearrange("p (n i) c -> p n c i", i=RUN),
                 in_=planes_of[batch_tile][:, :, cols].rearrange("p c (n i) -> p n c i", i=RUN),
             )
             nc.sync.dma_start(out=out[rows, cols, :], in_=woven[:])
 
-        for i in range(len(grad_steps) + EMPTY_LAG + chunks):
-            if i < len(grad_steps):
-                batch_tile, first, count = grad_steps[i]
-                if first == 0 and batch_tile + AHEAD < batch_tiles:
-                    grad_raws[batch_tile + AHEAD] = load_grad(batch_tile + AHEAD)
-                grouped_of[i] = regroup(grad_raws[batch_tile], first, count)
-            q = i - QUANTISE_LAG
-            if 0 <= q < len(grad_steps):
-                quantise_and_multiply(q)
-            e = i - EMPTY_LAG
-            if 0 <= e < len(grad_steps):
-                empty_banks(e)
-            if e >= len(groups) and e % len(groups) < chunks:
-                weave_and_store(e // len(groups) - 1, e % len(groups))
+        psi_steps = sum(1 for step in steps if not step[0])
+        quantised_in = {}
+        weaves = []
+        done = {"quantised": 0, "emptied": psi_steps, "woven": 0}
+
+        def one_round(n):
+            if n < len(copies):
+                step, part, on_vector = copies[n]
+                is_grad, tile, first, count = steps[step]
+                regroup(step, part, on_vector)
+                if is_grad and last_copy[step] == n and first + count == BLOCKS and tile + AHEAD + 1 < batch_tiles:
+                    load(True, tile + AHEAD + 1)
+            for step in range(done["quantised"], len(steps)):
+                if last_copy[step] + QUANTISE_LAG <= n:
+                    if steps[step][0]:
+                        quantise_and_multiply(step)
+                    else:
+                        quantise_psi(step)
+                    quantised_in[step] = n
+                    done["quantised"] = step + 1
+            if done["woven"] < len(weaves):
+                weave_and_store(*weaves[done["woven"]])
+                done["woven"] += 1
+            for step in range(done["emptied"], done["quantised"]):
+                if quantised_in[step] + EMPTY_LAG <= n:
+                    empty_banks(step)
+                    is_grad, tile, first, count = steps[step]
+                    if first + count == BLOCKS:
+                        weaves.extend((tile, chunk) for chunk in range(chunks))
+                    done["emptied"] = step + 1
+
+        with tc.tile_pool(name="psi_in", bufs=chunks) as psi_in:
+            pools["psi_in"] = psi_in
+            for chunk in range(chunks):
+                load(False, chunk)
+            for batch_tile in range(AHEAD + 1):
+                load(True, batch_tile)
+            for n in range(psi_copies):
+                one_round(n)
+        pools["plane"] = ctx.enter_context(tc.tile_pool(name="plane_pool", bufs=2))
+        pools["out"] = ctx.enter_context(tc.tile_pool(name="out_pool", bufs=4))
+        for n in range(psi_copies, len(copies) + QUANTISE_LAG + EMPTY_LAG + chunks + 1):
+            one_round(n)

@@ -22,6 +22,11 @@ COLS = 128
 RUN = 4
 QUANTISE_LAG = 2
 EMPTY_LAG = 2
+PSI_RUNS = ((0, 4, "V"), (4, 4, "S"), (8, 1, "S"))
+GRAD_ROUTES = "VSVSVSVSV"
+LEAD = {"V": 0, "S": 2}
+WEAVE_LAG = 2
+WEAVE_STEP = 2
 AHEAD = 2
 
 SCALE = 1.0 / math.sqrt(IN_FEATURES)
@@ -55,24 +60,31 @@ def tile_s2conv_pa_kernel(tc, x, psi, grad_out, out):
     whole = [slice(0, COLS)]
 
     steps = []
-    copies = []
-    for is_grad, tiles, planes in ((False, chunks, COEFFS), (True, batch_tiles, BLOCKS)):
-        groups = plane_groups(planes)
+    events = []
+    grad_runs = tuple((first, count, GRAD_ROUTES[n]) for n, (first, count) in enumerate(plane_groups(BLOCKS)))
+    place = 0
+    for is_grad, tiles, runs in ((False, chunks, PSI_RUNS), (True, batch_tiles, grad_runs)):
         for tile in range(tiles):
             base = len(steps)
-            for first, count in groups:
+            for first, count, route in runs:
                 steps.append((is_grad, tile, first, count))
-            for part in halves if tile == 0 else whole:
-                for n in range(len(groups)):
-                    if is_grad:
-                        on_vector = n % 2 == 0
-                    else:
-                        on_vector = n == 0
-                    copies.append((base + n, part, on_vector))
-    last_copy = {}
-    for n, (step, part, on_vector) in enumerate(copies):
-        last_copy[step] = n
-    psi_copies = sum(1 for step, part, on_vector in copies if not steps[step][0])
+            parts = halves if tile == 0 else whole
+            for part in parts:
+                for n, (first, count, route) in enumerate(runs):
+                    events.append((place - LEAD[route], len(events), "copy", (base + n, part, route)))
+                    if part == parts[-1]:
+                        events.append((place + QUANTISE_LAG, len(events), "quantise", (base + n,)))
+                        if is_grad:
+                            events.append((place + QUANTISE_LAG + EMPTY_LAG, len(events), "empty", (base + n,)))
+                    place += 1
+            if is_grad:
+                if tile + AHEAD + 1 < batch_tiles:
+                    events.append((place - 0.5, len(events), "load", (True, tile + AHEAD + 1)))
+                for chunk in range(chunks):
+                    events.append((place + QUANTISE_LAG + EMPTY_LAG + WEAVE_LAG + WEAVE_STEP * chunk, len(events), "weave", (tile, chunk)))
+            elif tile == chunks - 1:
+                events.append((place - 0.5, len(events), "psi done", ()))
+    events = sorted(events)
 
     with ExitStack() as ctx:
         ctx.enter_context(tc.manual_schedule())
@@ -103,12 +115,12 @@ def tile_s2conv_pa_kernel(tc, x, psi, grad_out, out):
                 cols = slice(tile * COLS + part.start, tile * COLS + part.stop)
                 nc.sync.dma_start(out=raw[:, :, part, :], in_=rows[:, :, cols, :])
 
-        def regroup(step, part, on_vector):
+        def regroup(step, part, route):
             is_grad, tile, first, count = steps[step]
             if step not in grouped_of:
                 grouped = group_pool.tile([P, RUN, COLS, PACK], BF16, align_bytes=64, name="grouped")
                 grouped_of[step] = grouped
-            copy = nc.vector.tensor_copy if on_vector else nc.scalar.copy
+            copy = nc.vector.tensor_copy if route == "V" else nc.scalar.copy
             copy(
                 out=grouped_of[step][:, 0:count, part].rearrange("p j c t -> p c t j"),
                 in_=raw_of[(is_grad, tile)][:, :, part, first : first + count].rearrange("p t c j -> p c t j"),
@@ -154,6 +166,12 @@ def tile_s2conv_pa_kernel(tc, x, psi, grad_out, out):
                     stop=closes,
                 )
 
+        def quantise(step):
+            if steps[step][0]:
+                quantise_and_multiply(step)
+            else:
+                quantise_psi(step)
+
         def empty_banks(step):
             is_grad, batch_tile, first, count = steps[step]
             if first == 0:
@@ -179,46 +197,23 @@ def tile_s2conv_pa_kernel(tc, x, psi, grad_out, out):
             )
             nc.sync.dma_start(out=out[rows, cols, :], in_=woven[:])
 
-        psi_steps = sum(1 for step in steps if not step[0])
-        quantised_in = {}
-        weaves = []
-        done = {"quantised": 0, "emptied": psi_steps, "woven": 0}
-
-        def one_round(n):
-            if n < len(copies):
-                step, part, on_vector = copies[n]
-                is_grad, tile, first, count = steps[step]
-                regroup(step, part, on_vector)
-                if is_grad and last_copy[step] == n and first + count == BLOCKS and tile + AHEAD + 1 < batch_tiles:
-                    load(True, tile + AHEAD + 1)
-            for step in range(done["quantised"], len(steps)):
-                if last_copy[step] + QUANTISE_LAG <= n:
-                    if steps[step][0]:
-                        quantise_and_multiply(step)
-                    else:
-                        quantise_psi(step)
-                    quantised_in[step] = n
-                    done["quantised"] = step + 1
-            if done["woven"] < len(weaves):
-                weave_and_store(*weaves[done["woven"]])
-                done["woven"] += 1
-            for step in range(done["emptied"], done["quantised"]):
-                if quantised_in[step] + EMPTY_LAG <= n:
-                    empty_banks(step)
-                    is_grad, tile, first, count = steps[step]
-                    if first + count == BLOCKS:
-                        weaves.extend((tile, chunk) for chunk in range(chunks))
-                    done["emptied"] = step + 1
-
+        stages = {
+            "copy": regroup,
+            "quantise": quantise,
+            "empty": empty_banks,
+            "weave": weave_and_store,
+            "load": load,
+        }
+        split = [n for n, event in enumerate(events) if event[2] == "psi done"][0]
         with tc.tile_pool(name="psi_in", bufs=chunks) as psi_in:
             pools["psi_in"] = psi_in
             for chunk in range(chunks):
                 load(False, chunk)
             for batch_tile in range(AHEAD + 1):
                 load(True, batch_tile)
-            for n in range(psi_copies):
-                one_round(n)
+            for place, order, stage, arguments in events[:split]:
+                stages[stage](*arguments)
         pools["plane"] = ctx.enter_context(tc.tile_pool(name="plane_pool", bufs=2))
         pools["out"] = ctx.enter_context(tc.tile_pool(name="out_pool", bufs=4))
-        for n in range(psi_copies, len(copies) + QUANTISE_LAG + EMPTY_LAG + chunks + 1):
-            one_round(n)
+        for place, order, stage, arguments in events[split + 1 :]:
+            stages[stage](*arguments)

@@ -23,7 +23,7 @@ RUN = 4
 QUANTISE_LAG = 2
 EMPTY_LAG = 2
 PSI_RUNS = ((0, 4, "V"), (4, 4, "S"), (8, 1, "S"))
-GRAD_ROUTES = "VSVSVSVSV"
+GRAD_ROUTES = ("VSVSVSVSV", "VSVSVSVSB", "VSVSVSVSB", "VSVSVSVSB")
 LEAD = {"V": 0, "S": 2}
 WEAVE_LAG = 2
 WEAVE_STEP = 2
@@ -61,17 +61,22 @@ def tile_s2conv_pa_kernel(tc, x, psi, grad_out, out):
 
     steps = []
     events = []
-    grad_runs = tuple((first, count, GRAD_ROUTES[n]) for n, (first, count) in enumerate(plane_groups(BLOCKS)))
     place = 0
-    for is_grad, tiles, runs in ((False, chunks, PSI_RUNS), (True, batch_tiles, grad_runs)):
+    for is_grad, tiles in ((False, chunks), (True, batch_tiles)):
         for tile in range(tiles):
+            if is_grad:
+                runs = tuple((first, count, GRAD_ROUTES[tile][n]) for n, (first, count) in enumerate(plane_groups(BLOCKS)))
+            else:
+                runs = PSI_RUNS
             base = len(steps)
             for first, count, route in runs:
                 steps.append((is_grad, tile, first, count))
             parts = halves if tile == 0 else whole
             for part in parts:
                 for n, (first, count, route) in enumerate(runs):
-                    events.append((place - LEAD[route], len(events), "copy", (base + n, part, route)))
+                    shares = ((halves[0], "V"), (halves[1], "S")) if route == "B" else ((part, route),)
+                    for share, engine in shares:
+                        events.append((place - LEAD[engine], len(events), "copy", (base + n, share, engine)))
                     if part == parts[-1]:
                         events.append((place + QUANTISE_LAG, len(events), "quantise", (base + n,)))
                         if is_grad:

@@ -22,6 +22,7 @@ COLS = 128
 RUN = 4
 QUANTISE_LAG = 2
 EMPTY_LAG = 2
+SHARED = 96
 PSI_RUNS = ((0, 4, "V"), (4, 4, "S"), (8, 1, "S"))
 GRAD_ROUTES = ("VSVSVSVSV", "VSVSVSVSB", "VSVSVSVSB", "VSVSVSVSB")
 LEAD = {"V": 0, "S": 2}
@@ -74,7 +75,7 @@ def tile_s2conv_pa_kernel(tc, x, psi, grad_out, out):
             parts = halves if tile == 0 else whole
             for part in parts:
                 for n, (first, count, route) in enumerate(runs):
-                    shares = ((halves[0], "V"), (halves[1], "S")) if route == "B" else ((part, route),)
+                    shares = ((slice(0, SHARED), "V"), (slice(SHARED, COLS), "S")) if route == "B" else ((part, route),)
                     for share, engine in shares:
                         events.append((place - LEAD[engine], len(events), "copy", (base + n, share, engine)))
                     if part == parts[-1]:

@@ -28,6 +28,7 @@ GRAD_ROUTES = ("VSVSVSVSV", "VSVSVSVSB", "VSVSVSVSB", "VSVSVSVSB")
 LEAD = {"V": 0, "S": 2}
 WEAVE_LAG = 2
 WEAVE_STEP = 2
+PAD = 32
 AHEAD = 2
 
 SCALE = 1.0 / math.sqrt(IN_FEATURES)
@@ -111,10 +112,12 @@ def tile_s2conv_pa_kernel(tc, x, psi, grad_out, out):
 
         def load(is_grad, tile):
             if is_grad:
-                raw = grad_in.tile([P, PACK, COLS, BLOCKS], BF16, name="grad_raw")
+                padded = grad_in.tile([P, PACK, COLS * BLOCKS + PAD], BF16, name="grad_raw")
+                raw = padded[:, :, 0 : COLS * BLOCKS].rearrange("p t (c j) -> p t c j", j=BLOCKS)
                 rows = grad_rows
             else:
-                raw = pools["psi_in"].tile([P, PACK, COLS, COEFFS], BF16, name="psi_raw")
+                padded = pools["psi_in"].tile([P, PACK, COLS * COEFFS + PAD], BF16, name="psi_raw")
+                raw = padded[:, :, 0 : COLS * COEFFS].rearrange("p t (c j) -> p t c j", j=COEFFS)
                 rows = psi_rows
             raw_of[(is_grad, tile)] = raw
             for part in halves if tile == 0 else whole:
@@ -186,12 +189,15 @@ def tile_s2conv_pa_kernel(tc, x, psi, grad_out, out):
             for n in range(count):
                 coefficient, psi_plane, opens, closes = table[first + n]
                 if closes:
-                    nc.scalar.activation(
-                        out=planes_of[batch_tile][:, coefficient],
-                        in_=bank_of[(batch_tile, coefficient)][:],
-                        func=mybir.ActivationFunctionType.Copy,
-                        scale=SCALE,
-                    )
+                    pieces = chunks if (batch_tile == batch_tiles - 1 and coefficient == COEFFS - 1) else 1
+                    for piece in range(pieces):
+                        cols = slice(piece * IN_FEATURES // pieces, (piece + 1) * IN_FEATURES // pieces)
+                        nc.scalar.activation(
+                            out=planes_of[batch_tile][:, coefficient, cols],
+                            in_=bank_of[(batch_tile, coefficient)][:, cols],
+                            func=mybir.ActivationFunctionType.Copy,
+                            scale=SCALE,
+                        )
 
         def weave_and_store(batch_tile, chunk):
             rows = slice(batch_tile * COLS, (batch_tile + 1) * COLS)

@@ -184,8 +184,8 @@ def tile_s2conv_pa_kernel(tc, x, psi, grad_out, out):
         def empty_banks(step):
             is_grad, batch_tile, first, count = steps[step]
             if first == 0:
-                planes = pools["plane"].tile([P, COEFFS, IN_FEATURES], F32, name="planes")
-                planes_of[batch_tile] = planes
+                padded = pools["plane"].tile([P, COEFFS, IN_FEATURES + PAD // 2], F32, name="planes")
+                planes_of[batch_tile] = padded[:, :, 0:IN_FEATURES]
             for n in range(count):
                 coefficient, psi_plane, opens, closes = table[first + n]
                 if closes:

@@ -2,6 +2,7 @@ import math
 from contextlib import ExitStack
 
 import concourse.mybir as mybir
+from concourse.masks import make_identity
 
 BF16 = mybir.dt.bfloat16
 F32 = mybir.dt.float32
@@ -22,10 +23,12 @@ COLS = 128
 RUN = 4
 QUANTISE_LAG = 2
 EMPTY_LAG = 2
-SHARED = 96
-PSI_RUNS = ((0, 4, "V"), (4, 4, "S"), (8, 1, "S"))
-GRAD_ROUTES = ("VSVSVSVSV", "VSVSVSVSB", "VSVSVSVSB", "VSVSVSVSB")
-LEAD = {"V": 0, "S": 2}
+PSI_ROUTES = ("VTS", "VTS", "VTS", "VTS")
+GRAD_ROUTES = ("VSVTVSVTS", "VSVTVSVTS", "VSVTVSVTS", "VSVTVSVTS")
+LEAD = {"V": 0, "S": 2, "T": 2}
+TENSOR_LEAD = 4
+BANK_COLS = 64
+PASS_COLS = 32
 WEAVE_LAG = 2
 WEAVE_STEP = 2
 PAD = 32
@@ -66,19 +69,23 @@ def tile_s2conv_pa_kernel(tc, x, psi, grad_out, out):
     place = 0
     for is_grad, tiles in ((False, chunks), (True, batch_tiles)):
         for tile in range(tiles):
-            if is_grad:
-                runs = tuple((first, count, GRAD_ROUTES[tile][n]) for n, (first, count) in enumerate(plane_groups(BLOCKS)))
-            else:
-                runs = PSI_RUNS
+            routes = GRAD_ROUTES[tile] if is_grad else PSI_ROUTES[tile]
+            groups = plane_groups(BLOCKS if is_grad else COEFFS)
+            runs = tuple((first, count, routes[n]) for n, (first, count) in enumerate(groups))
             base = len(steps)
             for first, count, route in runs:
                 steps.append((is_grad, tile, first, count))
             parts = halves if tile == 0 else whole
             for part in parts:
                 for n, (first, count, route) in enumerate(runs):
-                    shares = ((slice(0, SHARED), "V"), (slice(SHARED, COLS), "S")) if route == "B" else ((part, route),)
-                    for share, engine in shares:
-                        events.append((place - LEAD[engine], len(events), "copy", (base + n, share, engine)))
+                    if route == "T":
+                        banks = [slice(c, c + BANK_COLS) for c in range(part.start, part.stop, BANK_COLS)]
+                        for bank_cols in banks:
+                            events.append((place - TENSOR_LEAD, len(events), "move", (base + n, bank_cols)))
+                        for bank_cols in banks:
+                            events.append((place - LEAD[route], len(events), "copy out", (base + n, bank_cols)))
+                    else:
+                        events.append((place - LEAD[route], len(events), "copy", (base + n, part, route)))
                     if part == parts[-1]:
                         events.append((place + QUANTISE_LAG, len(events), "quantise", (base + n,)))
                         if is_grad:
@@ -99,13 +106,18 @@ def tile_s2conv_pa_kernel(tc, x, psi, grad_out, out):
         grad_in = ctx.enter_context(tc.tile_pool(name="grad_in", bufs=AHEAD + 1))
         group_pool = ctx.enter_context(tc.tile_pool(name="group_pool", bufs=10))
         code_pool = ctx.enter_context(tc.tile_pool(name="code_pool", bufs=4))
-        psum = ctx.enter_context(tc.psum_pool(name="psum", bufs=8))
+        psum = ctx.enter_context(tc.psum_pool(name="psum", bufs=6))
+        moved_pool = ctx.enter_context(tc.psum_pool(name="moved_pool", bufs=2))
+
+        identity = keep.tile([P, P], BF16, align_bytes=64, name="identity")
+        make_identity(nc, identity[:])
 
         psi_codes = keep.tile([P, COEFFS, IN_FEATURES], U32, align_bytes=64)
         psi_scales = keep.tile([P, COEFFS, IN_FEATURES], U8, align_bytes=64)
 
         raw_of = {}
         grouped_of = {}
+        moved_of = {}
         bank_of = {}
         planes_of = {}
         pools = {}
@@ -134,6 +146,26 @@ def tile_s2conv_pa_kernel(tc, x, psi, grad_out, out):
                 out=grouped_of[step][:, 0:count, part].rearrange("p j c t -> p c t j"),
                 in_=raw_of[(is_grad, tile)][:, :, part, first : first + count].rearrange("p t c j -> p c t j"),
             )
+
+        def move(step, part):
+            is_grad, tile, first, count = steps[step]
+            moved = moved_pool.tile([P, RUN, BANK_COLS, PACK], BF16, name="moved")
+            moved_of[(step, part.start)] = moved
+            for at in range(0, BANK_COLS, PASS_COLS):
+                cols = slice(part.start + at, part.start + at + PASS_COLS)
+                nc.tensor.matmul(
+                    out=moved[:, :, at : at + PASS_COLS].rearrange("p j c t -> p t c j"),
+                    lhsT=identity[:],
+                    rhs=raw_of[(is_grad, tile)][:, :, cols, first : first + count],
+                    start=True,
+                    stop=True,
+                )
+
+        def copy_out(step, part):
+            if step not in grouped_of:
+                grouped = group_pool.tile([P, RUN, COLS, PACK], BF16, align_bytes=64, name="grouped")
+                grouped_of[step] = grouped
+            nc.scalar.copy(out=grouped_of[step][:, :, part], in_=moved_of[(step, part.start)][:])
 
         def quantise_psi(step):
             is_grad, chunk, first, count = steps[step]
@@ -211,6 +243,8 @@ def tile_s2conv_pa_kernel(tc, x, psi, grad_out, out):
 
         stages = {
             "copy": regroup,
+            "move": move,
+            "copy out": copy_out,
             "quantise": quantise,
             "empty": empty_banks,
             "weave": weave_and_store,

@@ -23,15 +23,27 @@ COLS = 128
 RUN = 4
 QUANTISE_LAG = 2
 EMPTY_LAG = 2
-PSI_ROUTES = ("VTS", "VTS", "VTS", "VTS")
-GRAD_ROUTES = ("VSVTVSVTS", "VSVTVSVTS", "VSVTVSVTS", "VSVTVSVTS")
-LEAD = {"V": 0, "S": 2, "T": 2}
-TENSOR_LEAD = 4
-BANK_COLS = 64
-PASS_COLS = 32
+PAIR = 8
+BANK_COLS = 32
+PASS_COLS = 16
+PSI_MOVED = (0, 64, 64, 64)
+GRAD_MOVED = ((32, 32, 32, 32), (32, 32, 32, 32), (32, 32, 32, 32), (32, 32, 32, 32))
+PSI_ROUTES = ("VSV", "VSV", "VSV", "VSV")
+GRAD_ROUTES = ("VSVSVSVSV", "VSVVVSVSV", "VSVSVSVSV", "VSVVVSVSV")
+S_LEAD = 2
+LEAD = {"V": 0, "S": S_LEAD}
+TENSOR_LEAD = 3
+OUT_LEAD = 1
 WEAVE_LAG = 2
 WEAVE_STEP = 2
 PAD = 32
+PAIR_BUFS = 5
+SINGLE_BUFS = 2
+CODE_BUFS = 4
+MOVED_BANKS = 2
+OUT_BUFS = 4
+PSI_HALVED = (3, 0, 0, 0)
+GRAD_HALVED = (6, 2, 0, 0)
 AHEAD = 2
 
 SCALE = 1.0 / math.sqrt(IN_FEATURES)
@@ -70,27 +82,33 @@ def tile_s2conv_pa_kernel(tc, x, psi, grad_out, out):
     for is_grad, tiles in ((False, chunks), (True, batch_tiles)):
         for tile in range(tiles):
             routes = GRAD_ROUTES[tile] if is_grad else PSI_ROUTES[tile]
+            moved_cols = GRAD_MOVED[tile] if is_grad else (PSI_MOVED[tile],)
             groups = plane_groups(BLOCKS if is_grad else COEFFS)
             runs = tuple((first, count, routes[n]) for n, (first, count) in enumerate(groups))
             base = len(steps)
             for first, count, route in runs:
                 steps.append((is_grad, tile, first, count))
-            parts = halves if tile == 0 else whole
-            for part in parts:
-                for n, (first, count, route) in enumerate(runs):
-                    if route == "T":
-                        banks = [slice(c, c + BANK_COLS) for c in range(part.start, part.stop, BANK_COLS)]
-                        for bank_cols in banks:
-                            events.append((place - TENSOR_LEAD, len(events), "move", (base + n, bank_cols)))
-                        for bank_cols in banks:
-                            events.append((place - LEAD[route], len(events), "copy out", (base + n, bank_cols)))
-                    else:
-                        events.append((place - LEAD[route], len(events), "copy", (base + n, part, route)))
-                    if part == parts[-1]:
-                        events.append((place + QUANTISE_LAG, len(events), "quantise", (base + n,)))
-                        if is_grad:
-                            events.append((place + QUANTISE_LAG + EMPTY_LAG, len(events), "empty", (base + n,)))
-                    place += 1
+            halved = GRAD_HALVED[tile] if is_grad else PSI_HALVED[tile]
+            visits = [(n, part) for part in halves for n in range(halved)] + [(n, whole[0]) for n in range(halved, len(runs))]
+            for n, part in visits:
+                first, count, route = runs[n]
+                paired = count == RUN
+                begin = part.start
+                if paired:
+                    end = min(moved_cols[n // 2], part.stop)
+                    if n % 2 == 0:
+                        for k, at in enumerate(range(begin, end, BANK_COLS)):
+                            cols = slice(at, at + BANK_COLS)
+                            events.append((place - TENSOR_LEAD + k, len(events), "move", (base + n, cols)))
+                            events.append((place - OUT_LEAD + k, len(events), "copy out", (base + n, cols)))
+                    begin = max(begin, end)
+                if begin < part.stop:
+                    events.append((place - LEAD[route], len(events), "copy", (base + n, slice(begin, part.stop), route)))
+                if part.stop == COLS:
+                    events.append((place + QUANTISE_LAG, len(events), "quantise", (base + n,)))
+                    if is_grad:
+                        events.append((place + QUANTISE_LAG + EMPTY_LAG, len(events), "empty", (base + n,)))
+                place += 1
             if is_grad:
                 if tile + AHEAD + 1 < batch_tiles:
                     events.append((place - 0.5, len(events), "load", (True, tile + AHEAD + 1)))
@@ -104,10 +122,11 @@ def tile_s2conv_pa_kernel(tc, x, psi, grad_out, out):
         ctx.enter_context(tc.manual_schedule())
         keep = ctx.enter_context(tc.tile_pool(name="keep", bufs=1))
         grad_in = ctx.enter_context(tc.tile_pool(name="grad_in", bufs=AHEAD + 1))
-        group_pool = ctx.enter_context(tc.tile_pool(name="group_pool", bufs=10))
-        code_pool = ctx.enter_context(tc.tile_pool(name="code_pool", bufs=4))
-        psum = ctx.enter_context(tc.psum_pool(name="psum", bufs=6))
-        moved_pool = ctx.enter_context(tc.psum_pool(name="moved_pool", bufs=2))
+        pair_pool = ctx.enter_context(tc.tile_pool(name="pair_pool", bufs=PAIR_BUFS))
+        single_pool = ctx.enter_context(tc.tile_pool(name="single_pool", bufs=SINGLE_BUFS))
+        code_pool = ctx.enter_context(tc.tile_pool(name="code_pool", bufs=CODE_BUFS))
+        psum = ctx.enter_context(tc.psum_pool(name="psum", bufs=8 - MOVED_BANKS))
+        moved_pool = ctx.enter_context(tc.psum_pool(name="moved_pool", bufs=MOVED_BANKS))
 
         identity = keep.tile([P, P], BF16, align_bytes=64, name="identity")
         make_identity(nc, identity[:])
@@ -117,10 +136,12 @@ def tile_s2conv_pa_kernel(tc, x, psi, grad_out, out):
 
         raw_of = {}
         grouped_of = {}
+        pair_of = {}
         moved_of = {}
         bank_of = {}
         planes_of = {}
         pools = {}
+        last_woven = []
 
         def load(is_grad, tile):
             if is_grad:
@@ -132,15 +153,27 @@ def tile_s2conv_pa_kernel(tc, x, psi, grad_out, out):
                 raw = padded[:, :, 0 : COLS * COEFFS].rearrange("p t (c j) -> p t c j", j=COEFFS)
                 rows = psi_rows
             raw_of[(is_grad, tile)] = raw
-            for part in halves if tile == 0 else whole:
+            for part in halves if (GRAD_HALVED if is_grad else PSI_HALVED)[tile] else whole:
                 cols = slice(tile * COLS + part.start, tile * COLS + part.stop)
                 nc.sync.dma_start(out=raw[:, :, part, :], in_=rows[:, :, cols, :])
 
+        def make_grouped(step):
+            if step in grouped_of:
+                return
+            is_grad, tile, first, count = steps[step]
+            if count == RUN:
+                pair = pair_pool.tile([P, PAIR, COLS, PACK], BF16, align_bytes=64, name="pair")
+                early = step - (first // RUN) % 2
+                pair_of[early] = pair
+                grouped_of[early] = pair[:, 0:RUN]
+                grouped_of[early + 1] = pair[:, RUN:PAIR]
+            else:
+                single = single_pool.tile([P, BLOCKS % RUN, COLS, PACK], BF16, align_bytes=64, name="single")
+                grouped_of[step] = single[:]
+
         def regroup(step, part, route):
             is_grad, tile, first, count = steps[step]
-            if step not in grouped_of:
-                grouped = group_pool.tile([P, RUN, COLS, PACK], BF16, align_bytes=64, name="grouped")
-                grouped_of[step] = grouped
+            make_grouped(step)
             copy = nc.vector.tensor_copy if route == "V" else nc.scalar.copy
             copy(
                 out=grouped_of[step][:, 0:count, part].rearrange("p j c t -> p c t j"),
@@ -149,23 +182,21 @@ def tile_s2conv_pa_kernel(tc, x, psi, grad_out, out):
 
         def move(step, part):
             is_grad, tile, first, count = steps[step]
-            moved = moved_pool.tile([P, RUN, BANK_COLS, PACK], BF16, name="moved")
+            moved = moved_pool.tile([P, PAIR, BANK_COLS, PACK], BF16, name="moved")
             moved_of[(step, part.start)] = moved
             for at in range(0, BANK_COLS, PASS_COLS):
                 cols = slice(part.start + at, part.start + at + PASS_COLS)
                 nc.tensor.matmul(
                     out=moved[:, :, at : at + PASS_COLS].rearrange("p j c t -> p t c j"),
                     lhsT=identity[:],
-                    rhs=raw_of[(is_grad, tile)][:, :, cols, first : first + count],
+                    rhs=raw_of[(is_grad, tile)][:, :, cols, first : first + PAIR],
                     start=True,
                     stop=True,
                 )
 
         def copy_out(step, part):
-            if step not in grouped_of:
-                grouped = group_pool.tile([P, RUN, COLS, PACK], BF16, align_bytes=64, name="grouped")
-                grouped_of[step] = grouped
-            nc.scalar.copy(out=grouped_of[step][:, :, part], in_=moved_of[(step, part.start)][:])
+            make_grouped(step)
+            nc.scalar.copy(out=pair_of[step][:, :, part], in_=moved_of[(step, part.start)][:])
 
         def quantise_psi(step):
             is_grad, chunk, first, count = steps[step]
@@ -234,12 +265,19 @@ def tile_s2conv_pa_kernel(tc, x, psi, grad_out, out):
         def weave_and_store(batch_tile, chunk):
             rows = slice(batch_tile * COLS, (batch_tile + 1) * COLS)
             cols = slice(chunk * COLS, (chunk + 1) * COLS)
-            woven = pools["out"].tile([P, COLS, COEFFS], F32, name="woven")
+            if batch_tile == batch_tiles - 1:
+                if chunk == 0:
+                    grad_raw = grad_in.tile([P, chunks, COLS, COEFFS], F32, name="grad_raw")
+                    last_woven.append(grad_raw)
+                woven = last_woven[0][:, chunk]
+            else:
+                tile = pools["out"].tile([P, COLS, COEFFS], F32, name="woven")
+                woven = tile[:]
             nc.vector.tensor_copy(
-                out=woven[:].rearrange("p (n i) c -> p n c i", i=RUN),
+                out=woven.rearrange("p (n i) c -> p n c i", i=RUN),
                 in_=planes_of[batch_tile][:, :, cols].rearrange("p c (n i) -> p n c i", i=RUN),
             )
-            nc.sync.dma_start(out=out[rows, cols, :], in_=woven[:])
+            nc.sync.dma_start(out=out[rows, cols, :], in_=woven)
 
         stages = {
             "copy": regroup,
@@ -260,6 +298,6 @@ def tile_s2conv_pa_kernel(tc, x, psi, grad_out, out):
             for place, order, stage, arguments in events[:split]:
                 stages[stage](*arguments)
         pools["plane"] = ctx.enter_context(tc.tile_pool(name="plane_pool", bufs=2))
-        pools["out"] = ctx.enter_context(tc.tile_pool(name="out_pool", bufs=4))
+        pools["out"] = ctx.enter_context(tc.tile_pool(name="out_pool", bufs=OUT_BUFS))
         for place, order, stage, arguments in events[split + 1 :]:
             stages[stage](*arguments)

@@ -26,10 +26,10 @@ EMPTY_LAG = 2
 PAIR = 8
 BANK_COLS = 32
 PASS_COLS = 16
-PSI_MOVED = (0, 64, 64, 64)
-GRAD_MOVED = ((32, 32, 32, 32), (32, 32, 32, 32), (32, 32, 32, 32), (32, 32, 32, 32))
-PSI_ROUTES = ("VSV", "VSV", "VSV", "VSV")
-GRAD_ROUTES = ("VSVSVSVSV", "VSVVVSVSV", "VSVSVSVSV", "VSVVVSVSV")
+PSI_WIDE = 2
+GRAD_MOVED = ((0, 32, 32, 32), (0, 32, 32, 32), (0, 32, 32, 32), (0, 32, 32, 32))
+PSI_ROUTES = ("VSS", "VSS", "VSS", "VSS")
+GRAD_ROUTES = ("VSVSVSVSV", "VSVSVSVSV", "VSVSVSVSV", "VSVSVSVSV")
 S_LEAD = 2
 LEAD = {"V": 0, "S": S_LEAD}
 TENSOR_LEAD = 3
@@ -42,8 +42,8 @@ SINGLE_BUFS = 2
 CODE_BUFS = 4
 MOVED_BANKS = 2
 OUT_BUFS = 4
-PSI_HALVED = (3, 0, 0, 0)
-GRAD_HALVED = (6, 2, 0, 0)
+PSI_PARTS = (64, 128)
+GRAD_HALVED = (9, 0, 0, 0)
 AHEAD = 2
 
 SCALE = 1.0 / math.sqrt(IN_FEATURES)
@@ -76,20 +76,26 @@ def tile_s2conv_pa_kernel(tc, x, psi, grad_out, out):
     halves = [slice(0, COLS // 2), slice(COLS // 2, COLS)]
     whole = [slice(0, COLS)]
 
+    def parts_of(is_grad, tile):
+        if is_grad:
+            return halves if GRAD_HALVED[tile] else whole
+        edges = (0,) + PSI_PARTS if tile == 0 else (0, COLS)
+        return [slice(a, b) for a, b in zip(edges, edges[1:])]
+
     steps = []
     events = []
     place = 0
     for is_grad, tiles in ((False, chunks), (True, batch_tiles)):
         for tile in range(tiles):
             routes = GRAD_ROUTES[tile] if is_grad else PSI_ROUTES[tile]
-            moved_cols = GRAD_MOVED[tile] if is_grad else (PSI_MOVED[tile],)
+            moved_cols = GRAD_MOVED[tile] if is_grad else (0,)
             groups = plane_groups(BLOCKS if is_grad else COEFFS)
             runs = tuple((first, count, routes[n]) for n, (first, count) in enumerate(groups))
             base = len(steps)
             for first, count, route in runs:
                 steps.append((is_grad, tile, first, count))
-            halved = GRAD_HALVED[tile] if is_grad else PSI_HALVED[tile]
-            visits = [(n, part) for part in halves for n in range(halved)] + [(n, whole[0]) for n in range(halved, len(runs))]
+            halved = (GRAD_HALVED[tile] if is_grad else len(runs)) if len(parts_of(is_grad, tile)) > 1 else 0
+            visits = [(n, part) for part in parts_of(is_grad, tile) for n in range(halved)] + [(n, whole[0]) for n in range(halved, len(runs))]
             for n, part in visits:
                 first, count, route = runs[n]
                 paired = count == RUN
@@ -104,7 +110,7 @@ def tile_s2conv_pa_kernel(tc, x, psi, grad_out, out):
                     begin = max(begin, end)
                 if begin < part.stop:
                     events.append((place - LEAD[route], len(events), "copy", (base + n, slice(begin, part.stop), route)))
-                if part.stop == COLS:
+                if part.stop == COLS and (is_grad or tile % PSI_WIDE == PSI_WIDE - 1):
                     events.append((place + QUANTISE_LAG, len(events), "quantise", (base + n,)))
                     if is_grad:
                         events.append((place + QUANTISE_LAG + EMPTY_LAG, len(events), "empty", (base + n,)))
@@ -136,6 +142,7 @@ def tile_s2conv_pa_kernel(tc, x, psi, grad_out, out):
 
         raw_of = {}
         grouped_of = {}
+        psi_grouped = {}
         pair_of = {}
         moved_of = {}
         bank_of = {}
@@ -153,7 +160,7 @@ def tile_s2conv_pa_kernel(tc, x, psi, grad_out, out):
                 raw = padded[:, :, 0 : COLS * COEFFS].rearrange("p t (c j) -> p t c j", j=COEFFS)
                 rows = psi_rows
             raw_of[(is_grad, tile)] = raw
-            for part in halves if (GRAD_HALVED if is_grad else PSI_HALVED)[tile] else whole:
+            for part in parts_of(is_grad, tile):
                 cols = slice(tile * COLS + part.start, tile * COLS + part.stop)
                 nc.sync.dma_start(out=raw[:, :, part, :], in_=rows[:, :, cols, :])
 
@@ -161,7 +168,18 @@ def tile_s2conv_pa_kernel(tc, x, psi, grad_out, out):
             if step in grouped_of:
                 return
             is_grad, tile, first, count = steps[step]
-            if count == RUN:
+            if not is_grad:
+                group = (tile // PSI_WIDE, first)
+                if group not in psi_grouped:
+                    if count == RUN:
+                        pair = pair_pool.tile([P, RUN, PSI_WIDE * COLS, PACK], BF16, align_bytes=64, name="pair")
+                        psi_grouped[group] = pair[:]
+                    else:
+                        single = single_pool.tile([P, COEFFS % RUN, PSI_WIDE * COLS, PACK], BF16, align_bytes=64, name="single")
+                        psi_grouped[group] = single[:]
+                at = tile % PSI_WIDE * COLS
+                grouped_of[step] = psi_grouped[group][:, :, at : at + COLS]
+            elif count == RUN:
                 pair = pair_pool.tile([P, PAIR, COLS, PACK], BF16, align_bytes=64, name="pair")
                 early = step - (first // RUN) % 2
                 pair_of[early] = pair
@@ -200,12 +218,12 @@ def tile_s2conv_pa_kernel(tc, x, psi, grad_out, out):
 
         def quantise_psi(step):
             is_grad, chunk, first, count = steps[step]
-            cols = slice(chunk * COLS, (chunk + 1) * COLS)
+            cols = slice((chunk + 1 - PSI_WIDE) * COLS, (chunk + 1) * COLS)
             for n in range(count):
                 nc.vector.quantize_mx(
                     out=psi_codes[:, first + n, cols].bitcast(E4M3_X4),
                     scales=psi_scales[:, first + n, cols],
-                    in_=grouped_of[step][:, n].rearrange("p c t -> p (c t)"),
+                    in_=psi_grouped[(chunk // PSI_WIDE, first)][:, n].rearrange("p c t -> p (c t)"),
                 )
 
         def quantise_and_multiply(step):

@@ -265,17 +265,17 @@ def tile_s2conv_pa_kernel(tc, x, psi, grad_out, out):
         def empty_banks(step):
             is_grad, batch_tile, first, count = steps[step]
             if first == 0:
-                padded = pools["plane"].tile([P, COEFFS, IN_FEATURES + PAD // 2], F32, name="planes")
-                planes_of[batch_tile] = padded[:, :, 0:IN_FEATURES]
+                planes_of[batch_tile] = pools["plane"].tile([P, IN_FEATURES // RUN, COEFFS, RUN], F32, name="planes")
             for n in range(count):
                 coefficient, psi_plane, opens, closes = table[first + n]
                 if closes:
                     pieces = chunks if (batch_tile == batch_tiles - 1 and coefficient == COEFFS - 1) else 1
                     for piece in range(pieces):
                         cols = slice(piece * IN_FEATURES // pieces, (piece + 1) * IN_FEATURES // pieces)
+                        lines = slice(cols.start // RUN, cols.stop // RUN)
                         nc.scalar.activation(
-                            out=planes_of[batch_tile][:, coefficient, cols],
-                            in_=bank_of[(batch_tile, coefficient)][:, cols],
+                            out=planes_of[batch_tile][:, lines, coefficient],
+                            in_=bank_of[(batch_tile, coefficient)][:, cols].rearrange("p (n i) -> p n i", i=RUN),
                             func=mybir.ActivationFunctionType.Copy,
                             scale=SCALE,
                         )
@@ -293,7 +293,7 @@ def tile_s2conv_pa_kernel(tc, x, psi, grad_out, out):
                 woven = tile[:]
             nc.vector.tensor_copy(
                 out=woven.rearrange("p (n i) c -> p n c i", i=RUN),
-                in_=planes_of[batch_tile][:, :, cols].rearrange("p c (n i) -> p n c i", i=RUN),
+                in_=planes_of[batch_tile][:, cols.start // RUN : cols.stop // RUN],
             )
             nc.sync.dma_start(out=out[rows, cols, :], in_=woven)
 

@@ -24,12 +24,20 @@ RUN = 4
 QUANTISE_LAG = 2
 EMPTY_LAG = 2
 PAIR = 8
-BANK_COLS = 32
-PASS_COLS = 16
+BANK = 256
+PASSES = 2
 PSI_WIDE = 2
-GRAD_MOVED = ((0, 32, 32, 32), (0, 32, 32, 32), (0, 32, 32, 32), (0, 32, 32, 32))
+GM0 = (0, 8, 8, 8)
+GM1 = (0, 8, 8, 8)
+GM2 = (0, 8, 8, 8)
+GM3 = (0, 8, 8, 8)
+GRAD_MOVED = (GM0, GM1, GM2, GM3)
 PSI_ROUTES = ("VSS", "VSS", "VSS", "VSS")
-GRAD_ROUTES = ("VSVSVSVSV", "VSVSVSVSV", "VSVSVSVSV", "VSVSVSVSV")
+GR0 = "VSVSVSVSV"
+GR1 = "VSVSVSVSV"
+GR2 = "VSVSVSVSV"
+GR3 = "VSVSVSVSV"
+GRAD_ROUTES = (GR0, GR1, GR2, GR3)
 S_LEAD = 2
 LEAD = {"V": 0, "S": S_LEAD}
 TENSOR_LEAD = 3
@@ -41,9 +49,11 @@ PAIR_BUFS = 5
 SINGLE_BUFS = 2
 CODE_BUFS = 4
 MOVED_BANKS = 2
-OUT_BUFS = 4
+OUT_BUFS = 1
 PSI_PARTS = (64, 128)
-GRAD_HALVED = (9, 0, 0, 0)
+GRAD_HALVED = (9, 2, 0, 0)
+LAST_CHUNKS = (128, 256, 384, 512)
+CHUNKS = (128, 256, 384, 512)
 AHEAD = 2
 
 SCALE = 1.0 / math.sqrt(IN_FEATURES)
@@ -82,6 +92,10 @@ def tile_s2conv_pa_kernel(tc, x, psi, grad_out, out):
         edges = (0,) + PSI_PARTS if tile == 0 else (0, COLS)
         return [slice(a, b) for a, b in zip(edges, edges[1:])]
 
+    def pieces_of(tile):
+        ends = LAST_CHUNKS if tile == batch_tiles - 1 else CHUNKS
+        return [slice(a, b) for a, b in zip((0,) + tuple(ends), ends)]
+
     steps = []
     events = []
     place = 0
@@ -100,14 +114,15 @@ def tile_s2conv_pa_kernel(tc, x, psi, grad_out, out):
                 first, count, route = runs[n]
                 paired = count == RUN
                 begin = part.start
-                if paired:
-                    end = min(moved_cols[n // 2], part.stop)
+                if paired and begin == 0 and moved_cols[n // 2]:
+                    planes = moved_cols[n // 2]
+                    moved = slice(PAIR - planes, PAIR)
+                    cols = slice(0, BANK // planes)
                     if n % 2 == 0:
-                        for k, at in enumerate(range(begin, end, BANK_COLS)):
-                            cols = slice(at, at + BANK_COLS)
-                            events.append((place - TENSOR_LEAD + k, len(events), "move", (base + n, cols)))
-                            events.append((place - OUT_LEAD + k, len(events), "copy out", (base + n, cols)))
-                    begin = max(begin, end)
+                        events.append((place - TENSOR_LEAD, len(events), "move", (base + n, moved, cols)))
+                        events.append((place - OUT_LEAD, len(events), "copy out", (base + n, moved, cols)))
+                    if moved.start <= first % PAIR:
+                        begin = cols.stop
                 if begin < part.stop:
                     events.append((place - LEAD[route], len(events), "copy", (base + n, slice(begin, part.stop), route)))
                 if part.stop == COLS and (is_grad or tile % PSI_WIDE == PSI_WIDE - 1):
@@ -118,8 +133,8 @@ def tile_s2conv_pa_kernel(tc, x, psi, grad_out, out):
             if is_grad:
                 if tile + AHEAD + 1 < batch_tiles:
                     events.append((place - 0.5, len(events), "load", (True, tile + AHEAD + 1)))
-                for chunk in range(chunks):
-                    events.append((place + QUANTISE_LAG + EMPTY_LAG + WEAVE_LAG + WEAVE_STEP * chunk, len(events), "weave", (tile, chunk)))
+                for k, cols in enumerate(pieces_of(tile)):
+                    events.append((place + QUANTISE_LAG + EMPTY_LAG + WEAVE_LAG + WEAVE_STEP * k, len(events), "weave", (tile, cols)))
             elif tile == chunks - 1:
                 events.append((place - 0.5, len(events), "psi done", ()))
     events = sorted(events)
@@ -148,7 +163,7 @@ def tile_s2conv_pa_kernel(tc, x, psi, grad_out, out):
         bank_of = {}
         planes_of = {}
         pools = {}
-        last_woven = []
+        woven_of = {}
 
         def load(is_grad, tile):
             if is_grad:
@@ -198,23 +213,26 @@ def tile_s2conv_pa_kernel(tc, x, psi, grad_out, out):
                 in_=raw_of[(is_grad, tile)][:, :, part, first : first + count].rearrange("p t c j -> p c t j"),
             )
 
-        def move(step, part):
+        def move(step, moved, part):
             is_grad, tile, first, count = steps[step]
-            moved = moved_pool.tile([P, PAIR, BANK_COLS, PACK], BF16, name="moved")
-            moved_of[(step, part.start)] = moved
-            for at in range(0, BANK_COLS, PASS_COLS):
-                cols = slice(part.start + at, part.start + at + PASS_COLS)
+            planes = moved.stop - moved.start
+            width = part.stop - part.start
+            bank = moved_pool.tile([P, planes, width, PACK], BF16, name="moved")
+            moved_of[step] = bank
+            for n in range(PASSES):
+                at = slice(n * width // PASSES, (n + 1) * width // PASSES)
+                cols = slice(part.start + at.start, part.start + at.stop)
                 nc.tensor.matmul(
-                    out=moved[:, :, at : at + PASS_COLS].rearrange("p j c t -> p t c j"),
+                    out=bank[:, :, at].rearrange("p j c t -> p t c j"),
                     lhsT=identity[:],
-                    rhs=raw_of[(is_grad, tile)][:, :, cols, first : first + PAIR],
+                    rhs=raw_of[(is_grad, tile)][:, :, cols, first + moved.start : first + moved.stop],
                     start=True,
                     stop=True,
                 )
 
-        def copy_out(step, part):
+        def copy_out(step, moved, part):
             make_grouped(step)
-            nc.scalar.copy(out=pair_of[step][:, :, part], in_=moved_of[(step, part.start)][:])
+            nc.scalar.copy(out=pair_of[step][:, moved, part], in_=moved_of[step][:])
 
         def quantise_psi(step):
             is_grad, chunk, first, count = steps[step]
@@ -269,9 +287,8 @@ def tile_s2conv_pa_kernel(tc, x, psi, grad_out, out):
             for n in range(count):
                 coefficient, psi_plane, opens, closes = table[first + n]
                 if closes:
-                    pieces = chunks if (batch_tile == batch_tiles - 1 and coefficient == COEFFS - 1) else 1
-                    for piece in range(pieces):
-                        cols = slice(piece * IN_FEATURES // pieces, (piece + 1) * IN_FEATURES // pieces)
+                    last = batch_tile == batch_tiles - 1 and coefficient == COEFFS - 1
+                    for cols in pieces_of(batch_tile) if last else [slice(0, IN_FEATURES)]:
                         lines = slice(cols.start // RUN, cols.stop // RUN)
                         nc.scalar.activation(
                             out=planes_of[batch_tile][:, lines, coefficient],
@@ -280,17 +297,16 @@ def tile_s2conv_pa_kernel(tc, x, psi, grad_out, out):
                             scale=SCALE,
                         )
 
-        def weave_and_store(batch_tile, chunk):
+        def weave_and_store(batch_tile, cols):
             rows = slice(batch_tile * COLS, (batch_tile + 1) * COLS)
-            cols = slice(chunk * COLS, (chunk + 1) * COLS)
-            if batch_tile == batch_tiles - 1:
-                if chunk == 0:
-                    grad_raw = grad_in.tile([P, chunks, COLS, COEFFS], F32, name="grad_raw")
-                    last_woven.append(grad_raw)
-                woven = last_woven[0][:, chunk]
-            else:
-                tile = pools["out"].tile([P, COLS, COEFFS], F32, name="woven")
-                woven = tile[:]
+            if cols.start == 0:
+                if batch_tile:
+                    grad_raw = grad_in.tile([P, IN_FEATURES, COEFFS], F32, name="grad_raw")
+                    woven_of[batch_tile] = grad_raw
+                else:
+                    first = pools["out"].tile([P, IN_FEATURES, COEFFS], F32, name="first")
+                    woven_of[batch_tile] = first
+            woven = woven_of[batch_tile][:, cols]
             nc.vector.tensor_copy(
                 out=woven.rearrange("p (n i) c -> p n c i", i=RUN),
                 in_=planes_of[batch_tile][:, cols.start // RUN : cols.stop // RUN],

@@ -51,9 +51,11 @@ CODE_BUFS = 4
 MOVED_BANKS = 2
 OUT_BUFS = 1
 PSI_PARTS = (64, 128)
-GRAD_HALVED = (9, 2, 0, 0)
+GRAD_HALVED = (9, 0, 0, 0)
 LAST_CHUNKS = (128, 256, 384, 512)
 CHUNKS = (128, 256, 384, 512)
+PSI_MOVED = ((0,), (4,), (4,), (4,))
+PSI_SHARED = 2
 AHEAD = 2
 
 SCALE = 1.0 / math.sqrt(IN_FEATURES)
@@ -102,7 +104,7 @@ def tile_s2conv_pa_kernel(tc, x, psi, grad_out, out):
     for is_grad, tiles in ((False, chunks), (True, batch_tiles)):
         for tile in range(tiles):
             routes = GRAD_ROUTES[tile] if is_grad else PSI_ROUTES[tile]
-            moved_cols = GRAD_MOVED[tile] if is_grad else (0,)
+            moved_cols = GRAD_MOVED[tile] if is_grad else PSI_MOVED[tile]
             groups = plane_groups(BLOCKS if is_grad else COEFFS)
             runs = tuple((first, count, routes[n]) for n, (first, count) in enumerate(groups))
             base = len(steps)
@@ -123,8 +125,12 @@ def tile_s2conv_pa_kernel(tc, x, psi, grad_out, out):
                         events.append((place - OUT_LEAD, len(events), "copy out", (base + n, moved, cols)))
                     if moved.start <= first % PAIR:
                         begin = cols.stop
-                if begin < part.stop:
-                    events.append((place - LEAD[route], len(events), "copy", (base + n, slice(begin, part.stop), route)))
+                shares = ((begin, part.stop, route),)
+                if not is_grad and tile == PSI_SHARED and n == 0:
+                    shares = ((begin, COLS // 2, "V"), (COLS // 2, part.stop, "S"))
+                for first_col, end_col, engine in shares:
+                    if first_col < end_col:
+                        events.append((place - LEAD[engine], len(events), "copy", (base + n, slice(first_col, end_col), engine)))
                 if part.stop == COLS and (is_grad or tile % PSI_WIDE == PSI_WIDE - 1):
                     events.append((place + QUANTISE_LAG, len(events), "quantise", (base + n,)))
                     if is_grad:
@@ -232,7 +238,9 @@ def tile_s2conv_pa_kernel(tc, x, psi, grad_out, out):
 
         def copy_out(step, moved, part):
             make_grouped(step)
-            nc.scalar.copy(out=pair_of[step][:, moved, part], in_=moved_of[step][:])
+            make_grouped(step + 1)
+            target = pair_of[step][:, moved] if moved.start == 0 else grouped_of[step + 1][:]
+            nc.scalar.copy(out=target[:, :, part], in_=moved_of[step][:])
 
         def quantise_psi(step):
             is_grad, chunk, first, count = steps[step]

import math
from contextlib import ExitStack

import concourse.mybir as mybir
from concourse.masks import make_identity

BF16 = mybir.dt.bfloat16
F32 = mybir.dt.float32
U32 = mybir.dt.uint32
U8 = mybir.dt.uint8
E4M3_X4 = mybir.dt.float8_e4m3fn_x4
E5M2_X4 = mybir.dt.float8_e5m2_x4

P = 128
PACK = 4
OUT_FEATURES = 512
BATCH = 512
IN_FEATURES = 512
DEGREES = 3
COEFFS = 9
BLOCKS = 35
COLS = 128
RUN = 4
QUANTISE_LAG = 2
EMPTY_LAG = 2
PAIR = 8
BANK = 256
PASSES = 2
PSI_WIDE = 2
GM0 = (0, 8, 8, 8)
GM1 = (0, 8, 8, 8)
GM2 = (0, 8, 8, 8)
GM3 = (0, 8, 8, 8)
GRAD_MOVED = (GM0, GM1, GM2, GM3)
PSI_ROUTES = ("VSS", "VSS", "VSS", "VSS")
GR0 = "VSVSVSVSV"
GR1 = "VSVSVSVSV"
GR2 = "VSVSVSVSV"
GR3 = "VSVSVSVSV"
GRAD_ROUTES = (GR0, GR1, GR2, GR3)
S_LEAD = 2
LEAD = {"V": 0, "S": S_LEAD}
TENSOR_LEAD = 3
OUT_LEAD = 1
WEAVE_LAG = 2
WEAVE_STEP = 2
PAD = 32
PAIR_BUFS = 5
SINGLE_BUFS = 2
CODE_BUFS = 4
MOVED_BANKS = 2
OUT_BUFS = 1
PSI_PARTS = (64, 128)
GRAD_HALVED = (9, 0, 0, 0)
LAST_CHUNKS = (128, 256, 384, 512)
CHUNKS = (128, 256, 384, 512)
PSI_MOVED = ((0,), (4,), (4,), (4,))
PSI_SHARED = 2
AHEAD = 2

SCALE = 1.0 / math.sqrt(IN_FEATURES)
FLOPS = 2 * OUT_FEATURES * BATCH * IN_FEATURES * BLOCKS
BYTES = 2 * OUT_FEATURES * (IN_FEATURES * COEFFS + BATCH * BLOCKS) + 4 * BATCH * IN_FEATURES * COEFFS


def products():
    rows = []
    for degree in range(DEGREES):
        d = 2 * degree + 1
        s = degree * degree
        for u in range(d):
            for m in range(d):
                rows.append((s + u, s + m, m == 0, m == d - 1))
    return rows


def plane_groups(planes):
    return [(first, min(RUN, planes - first)) for first in range(0, planes, RUN)]


def tile_s2conv_pa_kernel(tc, x, psi, grad_out, out):
    nc = tc.nc
    psi_rows = psi.rearrange("(p t) f c -> p t f c", t=PACK)
    grad_rows = grad_out.rearrange("(p t) b j -> p t b j", t=PACK)
    chunks = IN_FEATURES // COLS
    batch_tiles = BATCH // COLS
    table = products()
    halves = [slice(0, COLS // 2), slice(COLS // 2, COLS)]
    whole = [slice(0, COLS)]

    def parts_of(is_grad, tile):
        if is_grad:
            return halves if GRAD_HALVED[tile] else whole
        edges = (0,) + PSI_PARTS if tile == 0 else (0, COLS)
        return [slice(a, b) for a, b in zip(edges, edges[1:])]

    def pieces_of(tile):
        ends = LAST_CHUNKS if tile == batch_tiles - 1 else CHUNKS
        return [slice(a, b) for a, b in zip((0,) + tuple(ends), ends)]

    steps = []
    events = []
    place = 0
    for is_grad, tiles in ((False, chunks), (True, batch_tiles)):
        for tile in range(tiles):
            routes = GRAD_ROUTES[tile] if is_grad else PSI_ROUTES[tile]
            moved_cols = GRAD_MOVED[tile] if is_grad else PSI_MOVED[tile]
            groups = plane_groups(BLOCKS if is_grad else COEFFS)
            runs = tuple((first, count, routes[n]) for n, (first, count) in enumerate(groups))
            base = len(steps)
            for first, count, route in runs:
                steps.append((is_grad, tile, first, count))
            halved = (GRAD_HALVED[tile] if is_grad else len(runs)) if len(parts_of(is_grad, tile)) > 1 else 0
            visits = [(n, part) for part in parts_of(is_grad, tile) for n in range(halved)] + [(n, whole[0]) for n in range(halved, len(runs))]
            for n, part in visits:
                first, count, route = runs[n]
                paired = count == RUN
                begin = part.start
                if paired and begin == 0 and moved_cols[n // 2]:
                    planes = moved_cols[n // 2]
                    moved = slice(PAIR - planes, PAIR)
                    cols = slice(0, BANK // planes)
                    if n % 2 == 0:
                        events.append((place - TENSOR_LEAD, len(events), "move", (base + n, moved, cols)))
                        events.append((place - OUT_LEAD, len(events), "copy out", (base + n, moved, cols)))
                    if moved.start <= first % PAIR:
                        begin = cols.stop
                shares = ((begin, part.stop, route),)
                if not is_grad and tile == PSI_SHARED and n == 0:
                    shares = ((begin, COLS // 2, "V"), (COLS // 2, part.stop, "S"))
                for first_col, end_col, engine in shares:
                    if first_col < end_col:
                        events.append((place - LEAD[engine], len(events), "copy", (base + n, slice(first_col, end_col), engine)))
                if part.stop == COLS and (is_grad or tile % PSI_WIDE == PSI_WIDE - 1):
                    events.append((place + QUANTISE_LAG, len(events), "quantise", (base + n,)))
                    if is_grad:
                        events.append((place + QUANTISE_LAG + EMPTY_LAG, len(events), "empty", (base + n,)))
                place += 1
            if is_grad:
                if tile + AHEAD + 1 < batch_tiles:
                    events.append((place - 0.5, len(events), "load", (True, tile + AHEAD + 1)))
                for k, cols in enumerate(pieces_of(tile)):
                    events.append((place + QUANTISE_LAG + EMPTY_LAG + WEAVE_LAG + WEAVE_STEP * k, len(events), "weave", (tile, cols)))
            elif tile == chunks - 1:
                events.append((place - 0.5, len(events), "psi done", ()))
    events = sorted(events)

    with ExitStack() as ctx:
        ctx.enter_context(tc.manual_schedule())
        keep = ctx.enter_context(tc.tile_pool(name="keep", bufs=1))
        grad_in = ctx.enter_context(tc.tile_pool(name="grad_in", bufs=AHEAD + 1))
        pair_pool = ctx.enter_context(tc.tile_pool(name="pair_pool", bufs=PAIR_BUFS))
        single_pool = ctx.enter_context(tc.tile_pool(name="single_pool", bufs=SINGLE_BUFS))
        code_pool = ctx.enter_context(tc.tile_pool(name="code_pool", bufs=CODE_BUFS))
        psum = ctx.enter_context(tc.psum_pool(name="psum", bufs=8 - MOVED_BANKS))
        moved_pool = ctx.enter_context(tc.psum_pool(name="moved_pool", bufs=MOVED_BANKS))

        identity = keep.tile([P, P], BF16, align_bytes=64, name="identity")
        make_identity(nc, identity[:])

        psi_codes = keep.tile([P, COEFFS, IN_FEATURES], U32, align_bytes=64)
        psi_scales = keep.tile([P, COEFFS, IN_FEATURES], U8, align_bytes=64)

        raw_of = {}
        grouped_of = {}
        psi_grouped = {}
        pair_of = {}
        moved_of = {}
        bank_of = {}
        planes_of = {}
        pools = {}
        woven_of = {}

        def load(is_grad, tile):
            if is_grad:
                padded = grad_in.tile([P, PACK, COLS * BLOCKS + PAD], BF16, name="grad_raw")
                raw = padded[:, :, 0 : COLS * BLOCKS].rearrange("p t (c j) -> p t c j", j=BLOCKS)
                rows = grad_rows
            else:
                padded = pools["psi_in"].tile([P, PACK, COLS * COEFFS + PAD], BF16, name="psi_raw")
                raw = padded[:, :, 0 : COLS * COEFFS].rearrange("p t (c j) -> p t c j", j=COEFFS)
                rows = psi_rows
            raw_of[(is_grad, tile)] = raw
            for part in parts_of(is_grad, tile):
                cols = slice(tile * COLS + part.start, tile * COLS + part.stop)
                nc.sync.dma_start(out=raw[:, :, part, :], in_=rows[:, :, cols, :])

        def make_grouped(step):
            if step in grouped_of:
                return
            is_grad, tile, first, count = steps[step]
            if not is_grad:
                group = (tile // PSI_WIDE, first)
                if group not in psi_grouped:
                    if count == RUN:
                        pair = pair_pool.tile([P, RUN, PSI_WIDE * COLS, PACK], BF16, align_bytes=64, name="pair")
                        psi_grouped[group] = pair[:]
                    else:
                        single = single_pool.tile([P, COEFFS % RUN, PSI_WIDE * COLS, PACK], BF16, align_bytes=64, name="single")
                        psi_grouped[group] = single[:]
                at = tile % PSI_WIDE * COLS
                grouped_of[step] = psi_grouped[group][:, :, at : at + COLS]
            elif count == RUN:
                pair = pair_pool.tile([P, PAIR, COLS, PACK], BF16, align_bytes=64, name="pair")
                early = step - (first // RUN) % 2
                pair_of[early] = pair
                grouped_of[early] = pair[:, 0:RUN]
                grouped_of[early + 1] = pair[:, RUN:PAIR]
            else:
                single = single_pool.tile([P, BLOCKS % RUN, COLS, PACK], BF16, align_bytes=64, name="single")
                grouped_of[step] = single[:]

        def regroup(step, part, route):
            is_grad, tile, first, count = steps[step]
            make_grouped(step)
            copy = nc.vector.tensor_copy if route == "V" else nc.scalar.copy
            copy(
                out=grouped_of[step][:, 0:count, part].rearrange("p j c t -> p c t j"),
                in_=raw_of[(is_grad, tile)][:, :, part, first : first + count].rearrange("p t c j -> p c t j"),
            )

        def move(step, moved, part):
            is_grad, tile, first, count = steps[step]
            planes = moved.stop - moved.start
            width = part.stop - part.start
            bank = moved_pool.tile([P, planes, width, PACK], BF16, name="moved")
            moved_of[step] = bank
            for n in range(PASSES):
                at = slice(n * width // PASSES, (n + 1) * width // PASSES)
                cols = slice(part.start + at.start, part.start + at.stop)
                nc.tensor.matmul(
                    out=bank[:, :, at].rearrange("p j c t -> p t c j"),
                    lhsT=identity[:],
                    rhs=raw_of[(is_grad, tile)][:, :, cols, first + moved.start : first + moved.stop],
                    start=True,
                    stop=True,
                )

        def copy_out(step, moved, part):
            make_grouped(step)
            make_grouped(step + 1)
            target = pair_of[step][:, moved] if moved.start == 0 else grouped_of[step + 1][:]
            nc.scalar.copy(out=target[:, :, part], in_=moved_of[step][:])

        def quantise_psi(step):
            is_grad, chunk, first, count = steps[step]
            cols = slice((chunk + 1 - PSI_WIDE) * COLS, (chunk + 1) * COLS)
            for n in range(count):
                nc.vector.quantize_mx(
                    out=psi_codes[:, first + n, cols].bitcast(E4M3_X4),
                    scales=psi_scales[:, first + n, cols],
                    in_=psi_grouped[(chunk // PSI_WIDE, first)][:, n].rearrange("p c t -> p (c t)"),
                )

        def quantise_and_multiply(step):
            is_grad, batch_tile, first, count = steps[step]
            grouped = grouped_of[step]
            codes = code_pool.tile([P, RUN, COLS], U32, align_bytes=64, name="codes")
            scales = code_pool.tile([P, RUN, COLS], U8, align_bytes=64, name="scales")
            done = 0
            for width in (4, 2, 1):
                if count - done >= width:
                    part = slice(done, done + width)
                    nc.vector.quantize_mx(
                        out=codes[:, part].rearrange("p j c -> p (j c)").bitcast(E5M2_X4),
                        scales=scales[:, part].rearrange("p j c -> p (j c)"),
                        in_=grouped[:, part].rearrange("p j c t -> p (j c t)"),
                    )
                    done += width
            for n in range(count):
                coefficient, psi_plane, opens, closes = table[first + n]
                if opens:
                    bank = psum.tile([P, IN_FEATURES], F32, name="bank")
                    bank_of[(batch_tile, coefficient)] = bank
                nc.tensor.matmul_mx(
                    out=bank_of[(batch_tile, coefficient)][:],
                    lhsT=codes[:, n].bitcast(E5M2_X4),
                    lhsT_scale=scales[:, n],
                    rhs=psi_codes[:, psi_plane].bitcast(E4M3_X4),
                    rhs_scale=psi_scales[:, psi_plane],
                    start=opens,
                    stop=closes,
                )

        def quantise(step):
            if steps[step][0]:
                quantise_and_multiply(step)
            else:
                quantise_psi(step)

        def empty_banks(step):
            is_grad, batch_tile, first, count = steps[step]
            if first == 0:
                planes_of[batch_tile] = pools["plane"].tile([P, IN_FEATURES // RUN, COEFFS, RUN], F32, name="planes")
            for n in range(count):
                coefficient, psi_plane, opens, closes = table[first + n]
                if closes:
                    last = batch_tile == batch_tiles - 1 and coefficient == COEFFS - 1
                    for cols in pieces_of(batch_tile) if last else [slice(0, IN_FEATURES)]:
                        lines = slice(cols.start // RUN, cols.stop // RUN)
                        nc.scalar.activation(
                            out=planes_of[batch_tile][:, lines, coefficient],
                            in_=bank_of[(batch_tile, coefficient)][:, cols].rearrange("p (n i) -> p n i", i=RUN),
                            func=mybir.ActivationFunctionType.Copy,
                            scale=SCALE,
                        )

        def weave_and_store(batch_tile, cols):
            rows = slice(batch_tile * COLS, (batch_tile + 1) * COLS)
            if cols.start == 0:
                if batch_tile:
                    grad_raw = grad_in.tile([P, IN_FEATURES, COEFFS], F32, name="grad_raw")
                    woven_of[batch_tile] = grad_raw
                else:
                    first = pools["out"].tile([P, IN_FEATURES, COEFFS], F32, name="first")
                    woven_of[batch_tile] = first
            woven = woven_of[batch_tile][:, cols]
            nc.vector.tensor_copy(
                out=woven.rearrange("p (n i) c -> p n c i", i=RUN),
                in_=planes_of[batch_tile][:, cols.start // RUN : cols.stop // RUN],
            )
            nc.sync.dma_start(out=out[rows, cols, :], in_=woven)

        stages = {
            "copy": regroup,
            "move": move,
            "copy out": copy_out,
            "quantise": quantise,
            "empty": empty_banks,
            "weave": weave_and_store,
            "load": load,
        }
        split = [n for n, event in enumerate(events) if event[2] == "psi done"][0]
        with tc.tile_pool(name="psi_in", bufs=chunks) as psi_in:
            pools["psi_in"] = psi_in
            for chunk in range(chunks):
                load(False, chunk)
            for batch_tile in range(AHEAD + 1):
                load(True, batch_tile)
            for place, order, stage, arguments in events[:split]:
                stages[stage](*arguments)
        pools["plane"] = ctx.enter_context(tc.tile_pool(name="plane_pool", bufs=2))
        pools["out"] = ctx.enter_context(tc.tile_pool(name="out_pool", bufs=OUT_BUFS))
        for place, order, stage, arguments in events[split + 1 :]:
            stages[stage](*arguments)
